import numpy as np
import ml_dtypes


def mxq(x, axis, fmt="e4m3"):
    dtype, down = {"e4m3": (ml_dtypes.float8_e4m3fn, 7), "e5m2": (ml_dtypes.float8_e5m2, 14)}[fmt]
    v = np.moveaxis(np.asarray(x, np.float32).astype(ml_dtypes.bfloat16).astype(np.float64), axis, -1)
    blocks = v.reshape(v.shape[:-1] + (-1, 32))
    amax = np.abs(blocks).max(-1, keepdims=True)
    byte = np.maximum(np.where(amax > 0, np.frexp(amax)[1] - 1 + 127, 0) - down, 1)
    scale = np.exp2(byte - 127.0)
    codes = (blocks / scale).astype(np.float32).astype(dtype).astype(np.float64)
    return np.moveaxis((codes * scale).reshape(v.shape), -1, axis)


WIDE = False


def mx_kscale(k):
    if not WIDE:
        return np.ones(k)
    levels = np.array([10, -10, 5, -5, 0])
    a = np.random.permutation(np.resize(levels, k // 512 * 4)).reshape(k // 512, 4)
    idx = np.arange(k)
    return np.exp2(a[idx // 512, idx % 128 // 32])


BF16 = ml_dtypes.bfloat16


def bf(x):
    return np.asarray(x, np.float32).astype(BF16)


def f64(x):
    return np.asarray(x).astype(np.float64)


E2M1 = np.array([0.0, 0.5, 1.0, 1.5, 2.0, 3.0, 4.0, 6.0, -0.0, -0.5, -1.0, -1.5, -2.0, -3.0, -4.0, -6.0])


def pack_weight(w, fmt):
    k, n = w.shape
    w = f64(bf(w)).reshape(k // 32, 32, n)
    amax = np.abs(w).max(1)
    if fmt == "e4m3":
        byte = np.frexp(amax)[1] - 1 + 127 - 7
    else:
        mant, ex = np.frexp(amax / 6.0)
        byte = np.where(mant > 0.5, ex, ex - 1) + 127
    byte = np.clip(np.where(amax > 0, byte, 1), 1, 254)
    scaled = (w * np.exp2(127.0 - byte)[:, None, :]).reshape(k, n).astype(np.float32)
    by_word = np.ascontiguousarray(scaled.reshape(k // 512, 128, 4, n).transpose(0, 1, 3, 2))
    if fmt == "e4m3":
        words = by_word.astype(ml_dtypes.float8_e4m3fn).view(np.uint8)
    else:
        c = by_word.astype(ml_dtypes.float4_e2m1fn).view(np.uint8) & 0xF
        words = c[..., 0::2] | (c[..., 1::2] << 4)
    return np.ascontiguousarray(words), np.ascontiguousarray(byte.astype(np.uint8).reshape(k // 512, 16, n))


def unpack_weight(words, scales, fmt):
    g, p, n, _ = words.shape
    if fmt == "e4m3":
        vals = np.ascontiguousarray(words).view(ml_dtypes.float8_e4m3fn).astype(np.float64)
    else:
        nib = np.empty((g, p, n, 4), np.uint8)
        nib[..., 0::2] = words & 0xF
        nib[..., 1::2] = words >> 4
        vals = E2M1[nib]
    vals = vals * np.repeat(np.exp2(scales.astype(np.float64) - 127.0), 8, axis=1)[..., None]
    return vals.transpose(0, 1, 3, 2).reshape(g * 512, n)


B, T, D, H, HD, F = 2, 64, 8192, 16, 64, 2048
A = H * HD
EPS = 1e-5
ERF_H = 0.5
ERF_N = 14
FMT = "e4m3"


def layernorm(x, g, b):
    mu = np.mean(x, axis=-1, keepdims=True)
    var = np.mean(np.square(x - mu), axis=-1, keepdims=True)
    return (x - mu) / np.sqrt(var + EPS) * g + b


def erf(z):
    acc = np.zeros_like(z)
    for n in range(ERF_N):
        tn = (n + 0.5) * ERF_H
        acc = acc + np.exp(-tn * tn) / (tn * tn + z * z)
    return np.tanh(np.pi * z / ERF_H) - 2.0 * ERF_H * z * np.exp(-z * z) / np.pi * acc


def gelu_erf(v):
    return 0.5 * v * (1.0 + erf(v / np.sqrt(2.0)))


def setup_inputs():
    s, t = mx_kscale(A), mx_kscale(D)
    attn = bf(np.random.standard_normal((B, T, A)) * 0.25 * s)
    x = bf(np.random.standard_normal((B, T, D)) + 0.5 * np.random.standard_normal((B, T, 1)))
    w_out_words, w_out_scales = pack_weight(np.random.standard_normal((A, D)) * 2.0 / np.sqrt(A) / s[:, None], FMT)
    b_out = bf(0.1 * np.random.standard_normal(D))
    ln2_g = bf((1.0 + 0.1 * np.random.standard_normal(D)) * t)
    ln2_b = bf(0.1 * np.random.standard_normal(D) * t)
    w1_words, w1_scales = pack_weight(np.random.standard_normal((D, F)) / np.sqrt(D) / t[:, None], FMT)
    b1 = bf(0.2 * np.random.standard_normal(F))
    return {"attn": attn,
            "x": x,
            "w_out_words": w_out_words,
            "w_out_scales": w_out_scales,
            "b_out": b_out,
            "ln2_g": ln2_g,
            "ln2_b": ln2_b,
            "w1_words": w1_words,
            "w1_scales": w1_scales,
            "b1": b1}


def reference(attn, x, w_out_words, w_out_scales, b_out, ln2_g, ln2_b, w1_words, w1_scales, b1):
    x_mid = f64(x) + ((mxq(f64(attn), 2, "e4m3") @ unpack_weight(w_out_words, w_out_scales, FMT)) + f64(b_out))
    h2 = layernorm(x_mid, f64(ln2_g), f64(ln2_b))
    hid = gelu_erf((mxq(h2, 2, "e4m3") @ unpack_weight(w1_words, w1_scales, FMT)) + f64(b1))
    return x_mid, hid

@@ -1,0 +1,279 @@
+from contextlib import ExitStack
+
+import concourse.mybir as mybir
+from concourse.masks import make_identity
+
+F32 = mybir.dt.float32
+BF16 = mybir.dt.bfloat16
+I32 = mybir.dt.int32
+U32 = mybir.dt.uint32
+U8 = mybir.dt.uint8
+FP8X4 = mybir.dt.float8_e4m3fn_x4
+ALU = mybir.AluOpType
+ACT = mybir.ActivationFunctionType
+
+P = 128
+PACK = 4
+K_PASS = P * PACK
+BANK = 512
+A_DIM = 1024
+D = 8192
+F = 2048
+EPS = 1e-5
+A_GROUPS = A_DIM // K_PASS
+D_GROUPS = D // K_PASS
+CHUNK = 2048
+CHUNK_BANKS = CHUNK // BANK
+WO_STRETCHES = D // CHUNK
+W_BUFS = 12
+ROUND = 2
+N_ROUNDS = D_GROUPS // ROUND
+ROW_B_OUT = 0
+ROW_B1 = 16
+ROW_GAIN = 32
+ROW_SHIFT = 48
+
+FLOPS = 2 * P * A_DIM * D + 2 * P * D * F
+
+
+def tile_transformerblock_pb_k_kernel(
+    tc, attn, x, w_out_words, w_out_scales, b_out, ln2_g, ln2_b, w1_words, w1_scales, b1, out_0, out_1
+):
+    nc = tc.nc
+    attn_rows = attn.flatten_outer_dims()
+    x_rows = x.flatten_outer_dims()
+    x_mid_out = out_0.flatten_outer_dims()
+    hid_out = out_1.flatten_outer_dims()
+    wo_words = w_out_words.rearrange("g p n t -> g p (n t)").bitcast(I32)
+    w1_words_i = w1_words.rearrange("g p n t -> g p (n t)").bitcast(I32)
+    wo_scales = w_out_scales.bitcast(I32)
+    w1_scales_i = w1_scales.bitcast(I32)
+
+    with ExitStack() as stack:
+        keep = stack.enter_context(tc.tile_pool(name="keep", bufs=1))
+        weights = stack.enter_context(tc.tile_pool(name="weights", bufs=W_BUFS))
+        work = stack.enter_context(tc.tile_pool(name="work", bufs=3))
+        psum = stack.enter_context(tc.psum_pool(name="psum", bufs=8))
+        stack.enter_context(tc.manual_schedule())
+
+        eps_col = keep.tile([P, 1], F32)
+        nc.vector.memset(eps_col[:], EPS)
+        table_warm = keep.tile([P, 1], F32)
+        nc.scalar.activation(out=table_warm[:], in_=eps_col[:], func=ACT.Sqrt)
+        vec_rows = keep.tile([P, BANK], BF16)
+        nc.vector.memset(vec_rows[:].bitcast(I32), 0)
+        wo_planes = keep.tile([P, A_GROUPS, CHUNK], U8, align_bytes=64)
+        nc.vector.memset(wo_planes[:].bitcast(I32), 0)
+        w1_planes = keep.tile([P, D_GROUPS // 4, F], U8, align_bytes=64)
+        nc.vector.memset(w1_planes[:].bitcast(I32), 0)
+        ident_f32 = keep.tile([P, P], F32)
+        make_identity(nc, ident_f32[:])
+        ident_bf = keep.tile([P, P], BF16)
+        make_identity(nc, ident_bf[:])
+
+        attn_sb = keep.tile([P, A_DIM], BF16)
+        nc.sync.dma_start(out=attn_sb[:], in_=attn_rows)
+        for row, vec in ((ROW_B_OUT, b_out), (ROW_B1, b1), (ROW_GAIN, ln2_g), (ROW_SHIFT, ln2_b)):
+            as_rows = vec.rearrange("(r c) -> r c", c=BANK)
+            nc.sync.dma_start(out=vec_rows[row : row + as_rows.shape[0], :], in_=as_rows)
+        x_sb = keep.tile([P, D], BF16)
+        for c in range(WO_STRETCHES):
+            cols = slice(c * CHUNK, (c + 1) * CHUNK)
+            nc.sync.dma_start(out=x_sb[:, cols], in_=x_rows[:, cols])
+        wo_planes_i = wo_planes[:].bitcast(I32)
+        for g in range(A_GROUPS):
+            for q in range(4):
+                nc.sync.dma_start(
+                    out=wo_planes_i[32 * q : 32 * q + 16, g, :],
+                    in_=wo_scales[g, 4 * q : 4 * q + 4, :].rearrange("r (c n) -> c r n", c=WO_STRETCHES),
+                )
+        w1_planes_i = w1_planes[:].bitcast(I32)
+        for four in range(D_GROUPS // 4):
+            for q in range(4):
+                nc.sync.dma_start(
+                    out=w1_planes_i[32 * q : 32 * q + 16, four, :],
+                    in_=w1_scales_i[4 * four : 4 * four + 4, 4 * q : 4 * q + 4, :],
+                )
+
+        chunk_sources = [
+            wo_words[g, :, c * CHUNK : (c + 1) * CHUNK] for c in range(WO_STRETCHES) for g in range(A_GROUPS)
+        ] + [w1_words_i[g] for g in range(D_GROUPS)]
+        chunks = []
+
+        def load_next_chunk():
+            if len(chunks) < len(chunk_sources):
+                words = weights.tile([P, CHUNK], U32, name="words", align_bytes=64)
+                nc.sync.dma_start(out=words[:].bitcast(I32), in_=chunk_sources[len(chunks)])
+                chunks.append(words)
+
+        for i in range(W_BUFS):
+            load_next_chunk()
+
+        attn_words = attn_sb[:].bitcast(F32)
+        attn_t = psum.tile([P, A_GROUPS, 2, P], F32, name="attn_t", tag="bank")
+        for g in range(A_GROUPS):
+            for u in range(2):
+                nc.tensor.transpose(
+                    out=attn_t[:, g, u, :],
+                    in_=attn_words[:, 256 * g + u : 256 * (g + 1) : 2],
+                    identity=ident_f32[:],
+                )
+        attn_grouped = keep.tile([P, A_GROUPS * P * PACK], BF16, align_bytes=64)
+        nc.vector.tensor_copy(
+            out=attn_grouped[:].bitcast(F32).rearrange("p (g k u) -> p g k u", g=A_GROUPS, u=2),
+            in_=attn_t[:].rearrange("p g u k -> p g k u"),
+        )
+        attn_codes = keep.tile([P, A_GROUPS * P], U32, align_bytes=64)
+        attn_plane = keep.tile([P, A_GROUPS * P], U8, align_bytes=64)
+
+        ln_t = psum.tile([P, PACK, P], BF16, name="ln_t", tag="bank")
+        for t in range(PACK):
+            nc.tensor.transpose(out=ln_t[:, t, :], in_=vec_rows[:, t:BANK:PACK], identity=ident_bf[:])
+        ln_cols = keep.tile([P, 2 * D_GROUPS, PACK], F32)
+        nc.vector.tensor_copy(
+            out=ln_cols[:], in_=ln_t[:, :, ROW_GAIN : ROW_GAIN + 2 * D_GROUPS].rearrange("p t r -> p r t")
+        )
+        nc.vector.quantize_mx(out=attn_codes[:].bitcast(FP8X4), scales=attn_plane[:], in_=attn_grouped[:])
+
+        def spread_row(row):
+            bank = psum.tile([P, BANK], F32, name="spread", tag="bank")
+            nc.tensor.matmul(
+                out=bank[:],
+                lhsT=ident_bf[:, row : row + 1].to_broadcast([P, P]),
+                rhs=vec_rows[:],
+                start=True,
+                stop=True,
+            )
+            return bank
+
+        x_mid = keep.tile([P, D], F32)
+        for j in range(D // BANK):
+            cols = slice(j * BANK, (j + 1) * BANK)
+            bank = spread_row(ROW_B_OUT + j)
+            nc.vector.tensor_tensor(out=x_mid[:, cols], in0=bank[:], in1=x_sb[:, cols], op=ALU.add)
+        b1_all = keep.tile([P, F], F32)
+        for j in range(F // BANK):
+            bank = spread_row(ROW_B1 + j)
+            nc.scalar.copy(out=b1_all[:, j * BANK : (j + 1) * BANK], in_=bank[:])
+
+        stats = keep.tile([P, D // BANK, 6], F32)
+        for c in range(WO_STRETCHES):
+            banks = [psum.tile([P, BANK], F32, name="acc%d" % b, tag="bank") for b in range(CHUNK_BANKS)]
+            for g in range(A_GROUPS):
+                words = chunks[c * A_GROUPS + g]
+                for b in range(CHUNK_BANKS):
+                    cols = slice(b * BANK, (b + 1) * BANK)
+                    nc.tensor.matmul_mx(
+                        out=banks[b][:],
+                        lhsT=attn_codes[:, g * P : (g + 1) * P].bitcast(FP8X4),
+                        lhsT_scale=attn_plane[:, g * P : (g + 1) * P],
+                        rhs=words[:, cols].bitcast(FP8X4),
+                        rhs_scale=wo_planes[4 * c : P, g, cols],
+                        start=(g == 0),
+                        stop=(g == A_GROUPS - 1),
+                    )
+                load_next_chunk()
+            for b in range(CHUNK_BANKS):
+                cols = slice(c * CHUNK + b * BANK, c * CHUNK + (b + 1) * BANK)
+                nc.vector.tensor_tensor(out=x_mid[:, cols], in0=banks[b][:], in1=x_mid[:, cols], op=ALU.add)
+            for b in range(CHUNK_BANKS):
+                cols = slice(c * CHUNK + b * BANK, c * CHUNK + (b + 1) * BANK)
+                nc.vector.bn_stats(out=stats[:, c * CHUNK_BANKS + b, :], in_=x_mid[:, cols])
+
+        mean_var = keep.tile([P, 2], F32)
+        nc.vector.bn_aggr(out=mean_var[:], in_=stats[:].rearrange("p j s -> p (j s)"))
+        std = keep.tile([P, 1], F32)
+        nc.scalar.activation(out=std[:], in_=mean_var[:, 1:2], func=ACT.Sqrt, bias=eps_col[:], scale=1.0)
+        rstd = keep.tile([P, 1], F32)
+        nc.vector.reciprocal(out=rstd[:], in_=std[:])
+        minus_mean_rstd = keep.tile([P, 1], F32)
+        nc.vector.tensor_scalar(
+            out=minus_mean_rstd[:], in0=mean_var[:, 0:1], scalar1=rstd[:, 0:1], scalar2=-1.0, op0=ALU.mult, op1=ALU.mult
+        )
+
+        h_codes = keep.tile([P, D_GROUPS * P], U32, align_bytes=64)
+        h_plane = keep.tile([P, D_GROUPS * P], U8, align_bytes=64)
+        hid_banks = [psum.tile([P, BANK], F32, name="hid%d" % b, tag="bank") for b in range(F // BANK)]
+        grouped_of_round = {}
+
+        def prepare(r):
+            groups = range(r * ROUND, (r + 1) * ROUND)
+            normed = {}
+            flipped = {}
+            scaled = {}
+            for g in groups:
+                normed[g] = work.tile([P, PACK, P], F32, name="normed", bufs=2 * ROUND)
+                nc.scalar.activation(
+                    out=normed[g][:].rearrange("k t p -> k p t"),
+                    in_=x_mid[:, g * K_PASS : (g + 1) * K_PASS].rearrange("k (p t) -> k p t", t=PACK),
+                    func=ACT.Identity,
+                    scale=rstd[:, 0:1],
+                    bias=minus_mean_rstd[:, 0:1],
+                )
+            for g in groups:
+                flipped[g] = psum.tile([P, PACK, P], F32, name="flipped", tag="bank")
+                for t in range(PACK):
+                    nc.tensor.transpose(out=flipped[g][:, t, :], in_=normed[g][:, t, :], identity=ident_f32[:])
+            for g in groups:
+                scaled[g] = work.tile([P, P, PACK], F32, name="scaled", bufs=2 * ROUND)
+                nc.vector.tensor_tensor(
+                    out=scaled[g][:],
+                    in0=flipped[g][:].rearrange("p t k -> p k t"),
+                    in1=ln_cols[:, g, :].unsqueeze(1).to_broadcast([P, P, PACK]),
+                    op=ALU.mult,
+                )
+            grouped = work.tile([P, ROUND, P, PACK], BF16, name="grouped", align_bytes=64)
+            for g in groups:
+                nc.vector.tensor_tensor(
+                    out=grouped[:, g - r * ROUND, :, :],
+                    in0=scaled[g][:],
+                    in1=ln_cols[:, D_GROUPS + g, :].unsqueeze(1).to_broadcast([P, P, PACK]),
+                    op=ALU.add,
+                )
+            grouped_of_round[r] = grouped
+
+        def quantise(r):
+            cols = slice(r * ROUND * P, (r + 1) * ROUND * P)
+            nc.vector.quantize_mx(
+                out=h_codes[:, cols].bitcast(FP8X4),
+                scales=h_plane[:, cols],
+                in_=grouped_of_round[r][:].rearrange("p g k t -> p (g k t)"),
+            )
+
+        def multiply(r):
+            for g in range(r * ROUND, (r + 1) * ROUND):
+                words = chunks[WO_STRETCHES * A_GROUPS + g]
+                for b in range(F // BANK):
+                    cols = slice(b * BANK, (b + 1) * BANK)
+                    nc.tensor.matmul_mx(
+                        out=hid_banks[b][:],
+                        lhsT=h_codes[:, g * P : (g + 1) * P].bitcast(FP8X4),
+                        lhsT_scale=h_plane[:, g * P : (g + 1) * P],
+                        rhs=words[:, cols].bitcast(FP8X4),
+                        rhs_scale=w1_planes[4 * (g % 4) : P, g // 4, cols],
+                        start=(g == 0),
+                        stop=(g == D_GROUPS - 1),
+                    )
+                load_next_chunk()
+
+        for r in range(N_ROUNDS + 2):
+            if r < N_ROUNDS:
+                prepare(r)
+            if 1 <= r <= N_ROUNDS:
+                quantise(r - 1)
+            if r >= 2:
+                multiply(r - 2)
+
+        for c in range(WO_STRETCHES):
+            cols = slice(c * CHUNK, (c + 1) * CHUNK)
+            nc.sync.dma_start(out=x_mid_out[:, cols], in_=x_mid[:, cols])
+
+        hid_sb = keep.tile([P, F], F32)
+        for b in range(F // BANK):
+            cols = slice(b * BANK, (b + 1) * BANK)
+            biased = work.tile([P, BANK], F32, name="biased")
+            nc.vector.tensor_tensor(out=biased[:], in0=hid_banks[b][:], in1=b1_all[:, cols], op=ALU.add)
+            nc.scalar.activation(out=hid_sb[:, cols], in_=biased[:], func=ACT.Gelu)
+        for half in range(2):
+            cols = slice(half * F // 2, (half + 1) * F // 2)
+            nc.sync.dma_start(out=hid_out[:, cols], in_=hid_sb[:, cols])

@@ -47,7 +47,7 @@ def tile_transformerblock_pb_k_kernel(
     wo_words = w_out_words.rearrange("g p n t -> g p (n t)").bitcast(I32)
     w1_words_i = w1_words.rearrange("g p n t -> g p (n t)").bitcast(I32)
     wo_scales = w_out_scales.bitcast(I32)
-    w1_scales_i = w1_scales.bitcast(I32)
+    w1_scales_f = w1_scales.bitcast(F32)
 
     with ExitStack() as stack:
         keep = stack.enter_context(tc.tile_pool(name="keep", bufs=1))
@@ -87,12 +87,12 @@ def tile_transformerblock_pb_k_kernel(
                     out=wo_planes_i[32 * q : 32 * q + 16, g, :],
                     in_=wo_scales[g, 4 * q : 4 * q + 4, :].rearrange("r (c n) -> c r n", c=WO_STRETCHES),
                 )
-        w1_planes_i = w1_planes[:].bitcast(I32)
+        w1_planes_f = w1_planes[:].bitcast(F32)
         for four in range(D_GROUPS // 4):
             for q in range(4):
-                nc.sync.dma_start(
-                    out=w1_planes_i[32 * q : 32 * q + 16, four, :],
-                    in_=w1_scales_i[4 * four : 4 * four + 4, 4 * q : 4 * q + 4, :],
+                nc.gpsimd.dma_start(
+                    out=w1_planes_f[32 * q : 32 * q + 16, four, :],
+                    in_=w1_scales_f[4 * four : 4 * four + 4, 4 * q : 4 * q + 4, :],
                 )
 
         chunk_sources = [

@@ -22,10 +22,12 @@ F = 2048
 EPS = 1e-5
 A_GROUPS = A_DIM // K_PASS
 D_GROUPS = D // K_PASS
-CHUNK = 2048
+CHUNK = 4096
 CHUNK_BANKS = CHUNK // BANK
-WO_STRETCHES = D // CHUNK
-W_BUFS = 12
+WO_HALVES = D // CHUNK
+STRETCH = F
+WO_STRETCHES = D // STRETCH
+W_BUFS = 6
 ROUND = 2
 N_ROUNDS = D_GROUPS // ROUND
 ROW_B_OUT = 0
@@ -56,13 +58,11 @@ def tile_transformerblock_pb_k_kernel(
         psum = stack.enter_context(tc.psum_pool(name="psum", bufs=8))
         stack.enter_context(tc.manual_schedule())
 
-        eps_col = keep.tile([P, 1], F32)
-        nc.vector.memset(eps_col[:], EPS)
-        table_warm = keep.tile([P, 1], F32)
-        nc.scalar.activation(out=table_warm[:], in_=eps_col[:], func=ACT.Sqrt)
         vec_rows = keep.tile([P, BANK], BF16)
         nc.vector.memset(vec_rows[:].bitcast(I32), 0)
-        wo_planes = keep.tile([P, A_GROUPS, CHUNK], U8, align_bytes=64)
+        eps_col = keep.tile([P, 1], F32)
+        nc.vector.memset(eps_col[:], EPS)
+        wo_planes = keep.tile([P, A_GROUPS, STRETCH], U8, align_bytes=64)
         nc.vector.memset(wo_planes[:].bitcast(I32), 0)
         w1_planes = keep.tile([P, D_GROUPS // 4, F], U8, align_bytes=64)
         nc.vector.memset(w1_planes[:].bitcast(I32), 0)
@@ -75,18 +75,20 @@ def tile_transformerblock_pb_k_kernel(
         nc.sync.dma_start(out=attn_sb[:], in_=attn_rows)
         for row, vec in ((ROW_B_OUT, b_out), (ROW_B1, b1), (ROW_GAIN, ln2_g), (ROW_SHIFT, ln2_b)):
             as_rows = vec.rearrange("(r c) -> r c", c=BANK)
-            nc.sync.dma_start(out=vec_rows[row : row + as_rows.shape[0], :], in_=as_rows)
+            nc.scalar.dma_start(out=vec_rows[row : row + as_rows.shape[0], :], in_=as_rows)
+        table_warm = keep.tile([P, 1], F32)
+        nc.scalar.activation(out=table_warm[:], in_=eps_col[:], func=ACT.Sqrt)
         x_sb = keep.tile([P, D], BF16)
-        for c in range(WO_STRETCHES):
-            cols = slice(c * CHUNK, (c + 1) * CHUNK)
-            nc.sync.dma_start(out=x_sb[:, cols], in_=x_rows[:, cols])
+        nc.sync.dma_start(out=x_sb[:], in_=x_rows)
         wo_planes_i = wo_planes[:].bitcast(I32)
-        for g in range(A_GROUPS):
+
+        def load_wo_scales(g):
             for q in range(4):
                 nc.sync.dma_start(
                     out=wo_planes_i[32 * q : 32 * q + 16, g, :],
                     in_=wo_scales[g, 4 * q : 4 * q + 4, :].rearrange("r (c n) -> c r n", c=WO_STRETCHES),
                 )
+
         w1_planes_f = w1_planes[:].bitcast(F32)
         for four in range(D_GROUPS // 4):
             for q in range(4):
@@ -96,17 +98,22 @@ def tile_transformerblock_pb_k_kernel(
                 )
 
         chunk_sources = [
-            wo_words[g, :, c * CHUNK : (c + 1) * CHUNK] for c in range(WO_STRETCHES) for g in range(A_GROUPS)
-        ] + [w1_words_i[g] for g in range(D_GROUPS)]
+            wo_words[g, :, h * CHUNK : (h + 1) * CHUNK].unsqueeze(1) for h in range(WO_HALVES) for g in range(A_GROUPS)
+        ] + [w1_words_i[r * ROUND : (r + 1) * ROUND].rearrange("g p n -> p g n") for r in range(N_ROUNDS)]
         chunks = []
 
         def load_next_chunk():
             if len(chunks) < len(chunk_sources):
                 words = weights.tile([P, CHUNK], U32, name="words", align_bytes=64)
-                nc.sync.dma_start(out=words[:].bitcast(I32), in_=chunk_sources[len(chunks)])
+                source = chunk_sources[len(chunks)]
+                nc.sync.dma_start(
+                    out=words[:].bitcast(I32).rearrange("p (g n) -> p g n", g=source.shape[1]), in_=source
+                )
                 chunks.append(words)
 
         for i in range(W_BUFS):
+            if i < A_GROUPS:
+                load_wo_scales(i)
             load_next_chunk()
 
         attn_words = attn_sb[:].bitcast(F32)
@@ -157,28 +164,29 @@ def tile_transformerblock_pb_k_kernel(
             nc.scalar.copy(out=b1_all[:, j * BANK : (j + 1) * BANK], in_=bank[:])
 
         stats = keep.tile([P, D // BANK, 6], F32)
-        for c in range(WO_STRETCHES):
+        for h in range(WO_HALVES):
             banks = [psum.tile([P, BANK], F32, name="acc%d" % b, tag="bank") for b in range(CHUNK_BANKS)]
             for g in range(A_GROUPS):
-                words = chunks[c * A_GROUPS + g]
+                words = chunks[h * A_GROUPS + g]
                 for b in range(CHUNK_BANKS):
                     cols = slice(b * BANK, (b + 1) * BANK)
+                    c, start_col = divmod(h * CHUNK + b * BANK, STRETCH)
                     nc.tensor.matmul_mx(
                         out=banks[b][:],
                         lhsT=attn_codes[:, g * P : (g + 1) * P].bitcast(FP8X4),
                         lhsT_scale=attn_plane[:, g * P : (g + 1) * P],
                         rhs=words[:, cols].bitcast(FP8X4),
-                        rhs_scale=wo_planes[4 * c : P, g, cols],
+                        rhs_scale=wo_planes[4 * c : P, g, start_col : start_col + BANK],
                         start=(g == 0),
                         stop=(g == A_GROUPS - 1),
                     )
                 load_next_chunk()
             for b in range(CHUNK_BANKS):
-                cols = slice(c * CHUNK + b * BANK, c * CHUNK + (b + 1) * BANK)
+                cols = slice(h * CHUNK + b * BANK, h * CHUNK + (b + 1) * BANK)
                 nc.vector.tensor_tensor(out=x_mid[:, cols], in0=banks[b][:], in1=x_mid[:, cols], op=ALU.add)
             for b in range(CHUNK_BANKS):
-                cols = slice(c * CHUNK + b * BANK, c * CHUNK + (b + 1) * BANK)
-                nc.vector.bn_stats(out=stats[:, c * CHUNK_BANKS + b, :], in_=x_mid[:, cols])
+                cols = slice(h * CHUNK + b * BANK, h * CHUNK + (b + 1) * BANK)
+                nc.vector.bn_stats(out=stats[:, h * CHUNK_BANKS + b, :], in_=x_mid[:, cols])
 
         mean_var = keep.tile([P, 2], F32)
         nc.vector.bn_aggr(out=mean_var[:], in_=stats[:].rearrange("p j s -> p (j s)"))
@@ -241,20 +249,21 @@ def tile_transformerblock_pb_k_kernel(
             )
 
         def multiply(r):
+            words = chunks[WO_HALVES * A_GROUPS + r]
             for g in range(r * ROUND, (r + 1) * ROUND):
-                words = chunks[WO_STRETCHES * A_GROUPS + g]
                 for b in range(F // BANK):
                     cols = slice(b * BANK, (b + 1) * BANK)
+                    first = (g - r * ROUND) * F + b * BANK
                     nc.tensor.matmul_mx(
                         out=hid_banks[b][:],
                         lhsT=h_codes[:, g * P : (g + 1) * P].bitcast(FP8X4),
                         lhsT_scale=h_plane[:, g * P : (g + 1) * P],
-                        rhs=words[:, cols].bitcast(FP8X4),
+                        rhs=words[:, first : first + BANK].bitcast(FP8X4),
                         rhs_scale=w1_planes[4 * (g % 4) : P, g // 4, cols],
                         start=(g == 0),
                         stop=(g == D_GROUPS - 1),
                     )
-                load_next_chunk()
+            load_next_chunk()
 
         for r in range(N_ROUNDS + 2):
             if r < N_ROUNDS:
@@ -264,9 +273,7 @@ def tile_transformerblock_pb_k_kernel(
             if r >= 2:
                 multiply(r - 2)
 
-        for c in range(WO_STRETCHES):
-            cols = slice(c * CHUNK, (c + 1) * CHUNK)
-            nc.sync.dma_start(out=x_mid_out[:, cols], in_=x_mid[:, cols])
+        nc.sync.dma_start(out=x_mid_out, in_=x_mid[:])
 
         hid_sb = keep.tile([P, F], F32)
         for b in range(F // BANK):
@@ -274,6 +281,4 @@ def tile_transformerblock_pb_k_kernel(
             biased = work.tile([P, BANK], F32, name="biased")
             nc.vector.tensor_tensor(out=biased[:], in0=hid_banks[b][:], in1=b1_all[:, cols], op=ALU.add)
             nc.scalar.activation(out=hid_sb[:, cols], in_=biased[:], func=ACT.Gelu)
-        for half in range(2):
-            cols = slice(half * F // 2, (half + 1) * F // 2)
-            nc.sync.dma_start(out=hid_out[:, cols], in_=hid_sb[:, cols])
+        nc.sync.dma_start(out=hid_out, in_=hid_sb[:])

@@ -22,12 +22,11 @@ F = 2048
 EPS = 1e-5
 A_GROUPS = A_DIM // K_PASS
 D_GROUPS = D // K_PASS
-CHUNK = 4096
+CHUNK = 2048
 CHUNK_BANKS = CHUNK // BANK
-WO_HALVES = D // CHUNK
-STRETCH = F
-WO_STRETCHES = D // STRETCH
-W_BUFS = 6
+WO_STRETCHES = D // CHUNK
+LEAD = 2
+W_BUFS = 10
 ROUND = 2
 N_ROUNDS = D_GROUPS // ROUND
 ROW_B_OUT = 0
@@ -62,7 +61,7 @@ def tile_transformerblock_pb_k_kernel(
         nc.vector.memset(vec_rows[:].bitcast(I32), 0)
         eps_col = keep.tile([P, 1], F32)
         nc.vector.memset(eps_col[:], EPS)
-        wo_planes = keep.tile([P, A_GROUPS, STRETCH], U8, align_bytes=64)
+        wo_planes = keep.tile([P, A_GROUPS, CHUNK], U8, align_bytes=64)
         nc.vector.memset(wo_planes[:].bitcast(I32), 0)
         w1_planes = keep.tile([P, D_GROUPS // 4, F], U8, align_bytes=64)
         nc.vector.memset(w1_planes[:].bitcast(I32), 0)
@@ -97,23 +96,22 @@ def tile_transformerblock_pb_k_kernel(
                     in_=w1_scales_f[4 * four : 4 * four + 4, 4 * q : 4 * q + 4, :],
                 )
 
+        lead_words = [keep.tile([P, LEAD * CHUNK], U32, name="lead%d" % g, align_bytes=64) for g in range(A_GROUPS)]
+        for g in range(A_GROUPS):
+            load_wo_scales(g)
+            nc.sync.dma_start(out=lead_words[g][:].bitcast(I32), in_=wo_words[g, :, : LEAD * CHUNK])
         chunk_sources = [
-            wo_words[g, :, h * CHUNK : (h + 1) * CHUNK].unsqueeze(1) for h in range(WO_HALVES) for g in range(A_GROUPS)
-        ] + [w1_words_i[r * ROUND : (r + 1) * ROUND].rearrange("g p n -> p g n") for r in range(N_ROUNDS)]
+            wo_words[g, :, c * CHUNK : (c + 1) * CHUNK] for c in range(LEAD, WO_STRETCHES) for g in range(A_GROUPS)
+        ] + [w1_words_i[g] for g in range(D_GROUPS)]
         chunks = []
 
         def load_next_chunk():
             if len(chunks) < len(chunk_sources):
                 words = weights.tile([P, CHUNK], U32, name="words", align_bytes=64)
-                source = chunk_sources[len(chunks)]
-                nc.sync.dma_start(
-                    out=words[:].bitcast(I32).rearrange("p (g n) -> p g n", g=source.shape[1]), in_=source
-                )
+                nc.sync.dma_start(out=words[:].bitcast(I32), in_=chunk_sources[len(chunks)])
                 chunks.append(words)
 
         for i in range(W_BUFS):
-            if i < A_GROUPS:
-                load_wo_scales(i)
             load_next_chunk()
 
         attn_words = attn_sb[:].bitcast(F32)
@@ -142,51 +140,62 @@ def tile_transformerblock_pb_k_kernel(
         )
         nc.vector.quantize_mx(out=attn_codes[:].bitcast(FP8X4), scales=attn_plane[:], in_=attn_grouped[:])
 
-        def spread_row(row):
-            bank = psum.tile([P, BANK], F32, name="spread", tag="bank")
+        def spread_row(bank, row, stop):
             nc.tensor.matmul(
                 out=bank[:],
                 lhsT=ident_bf[:, row : row + 1].to_broadcast([P, P]),
                 rhs=vec_rows[:],
                 start=True,
-                stop=True,
+                stop=stop,
             )
-            return bank
 
-        x_mid = keep.tile([P, D], F32)
-        for j in range(D // BANK):
-            cols = slice(j * BANK, (j + 1) * BANK)
-            bank = spread_row(ROW_B_OUT + j)
-            nc.vector.tensor_tensor(out=x_mid[:, cols], in0=bank[:], in1=x_sb[:, cols], op=ALU.add)
         b1_all = keep.tile([P, F], F32)
         for j in range(F // BANK):
-            bank = spread_row(ROW_B1 + j)
+            bank = psum.tile([P, BANK], F32, name="spread", tag="bank")
+            spread_row(bank, ROW_B1 + j, stop=True)
             nc.scalar.copy(out=b1_all[:, j * BANK : (j + 1) * BANK], in_=bank[:])
 
+        x_mid = keep.tile([P, D], F32)
+
+        def start_x_mid(c):
+            for j in range(c * CHUNK_BANKS, (c + 1) * CHUNK_BANKS):
+                cols = slice(j * BANK, (j + 1) * BANK)
+                bank = psum.tile([P, BANK], F32, name="spread", tag="bank")
+                spread_row(bank, ROW_B_OUT + j, stop=False)
+                nc.tensor.matmul(out=bank[:], lhsT=ident_bf[:], rhs=x_sb[:, cols], start=False, stop=True)
+                nc.scalar.copy(out=x_mid[:, cols], in_=bank[:])
+
+        start_x_mid(0)
+
         stats = keep.tile([P, D // BANK, 6], F32)
-        for h in range(WO_HALVES):
+        for c in range(WO_STRETCHES):
+            if c + 1 < WO_STRETCHES:
+                start_x_mid(c + 1)
             banks = [psum.tile([P, BANK], F32, name="acc%d" % b, tag="bank") for b in range(CHUNK_BANKS)]
             for g in range(A_GROUPS):
-                words = chunks[h * A_GROUPS + g]
                 for b in range(CHUNK_BANKS):
                     cols = slice(b * BANK, (b + 1) * BANK)
-                    c, start_col = divmod(h * CHUNK + b * BANK, STRETCH)
+                    if c < LEAD:
+                        rhs = lead_words[g][:, c * CHUNK + b * BANK : c * CHUNK + (b + 1) * BANK]
+                    else:
+                        rhs = chunks[(c - LEAD) * A_GROUPS + g][:, cols]
                     nc.tensor.matmul_mx(
                         out=banks[b][:],
                         lhsT=attn_codes[:, g * P : (g + 1) * P].bitcast(FP8X4),
                         lhsT_scale=attn_plane[:, g * P : (g + 1) * P],
-                        rhs=words[:, cols].bitcast(FP8X4),
-                        rhs_scale=wo_planes[4 * c : P, g, start_col : start_col + BANK],
+                        rhs=rhs.bitcast(FP8X4),
+                        rhs_scale=wo_planes[4 * c : P, g, cols],
                         start=(g == 0),
                         stop=(g == A_GROUPS - 1),
                     )
-                load_next_chunk()
+                if c >= LEAD:
+                    load_next_chunk()
             for b in range(CHUNK_BANKS):
-                cols = slice(h * CHUNK + b * BANK, h * CHUNK + (b + 1) * BANK)
+                cols = slice(c * CHUNK + b * BANK, c * CHUNK + (b + 1) * BANK)
                 nc.vector.tensor_tensor(out=x_mid[:, cols], in0=banks[b][:], in1=x_mid[:, cols], op=ALU.add)
             for b in range(CHUNK_BANKS):
-                cols = slice(h * CHUNK + b * BANK, h * CHUNK + (b + 1) * BANK)
-                nc.vector.bn_stats(out=stats[:, h * CHUNK_BANKS + b, :], in_=x_mid[:, cols])
+                cols = slice(c * CHUNK + b * BANK, c * CHUNK + (b + 1) * BANK)
+                nc.vector.bn_stats(out=stats[:, c * CHUNK_BANKS + b, :], in_=x_mid[:, cols])
 
         mean_var = keep.tile([P, 2], F32)
         nc.vector.bn_aggr(out=mean_var[:], in_=stats[:].rearrange("p j s -> p (j s)"))
@@ -202,42 +211,50 @@ def tile_transformerblock_pb_k_kernel(
         h_codes = keep.tile([P, D_GROUPS * P], U32, align_bytes=64)
         h_plane = keep.tile([P, D_GROUPS * P], U8, align_bytes=64)
         hid_banks = [psum.tile([P, BANK], F32, name="hid%d" % b, tag="bank") for b in range(F // BANK)]
+        normed_of_round = {}
+        flipped_of_round = {}
+        affine_of_round = {}
         grouped_of_round = {}
 
-        def prepare(r):
-            groups = range(r * ROUND, (r + 1) * ROUND)
-            normed = {}
-            flipped = {}
-            scaled = {}
-            for g in groups:
-                normed[g] = work.tile([P, PACK, P], F32, name="normed", bufs=2 * ROUND)
-                nc.scalar.activation(
-                    out=normed[g][:].rearrange("k t p -> k p t"),
-                    in_=x_mid[:, g * K_PASS : (g + 1) * K_PASS].rearrange("k (p t) -> k p t", t=PACK),
-                    func=ACT.Identity,
-                    scale=rstd[:, 0:1],
-                    bias=minus_mean_rstd[:, 0:1],
-                )
-            for g in groups:
-                flipped[g] = psum.tile([P, PACK, P], F32, name="flipped", tag="bank")
+        def normalise(r):
+            normed = work.tile([P, ROUND, PACK, P], F32, name="normed")
+            nc.vector.tensor_scalar(
+                out=normed[:].rearrange("k g t p -> k g p t"),
+                in0=x_mid[:, r * ROUND * K_PASS : (r + 1) * ROUND * K_PASS].rearrange(
+                    "k (g p t) -> k g p t", g=ROUND, t=PACK
+                ),
+                scalar1=rstd[:, 0:1],
+                scalar2=minus_mean_rstd[:, 0:1],
+                op0=ALU.mult,
+                op1=ALU.add,
+            )
+            normed_of_round[r] = normed
+
+        def flip(r):
+            flipped_of_round[r] = []
+            for i in range(ROUND):
+                flipped = psum.tile([P, PACK, P], F32, name="flipped", tag="bank")
                 for t in range(PACK):
-                    nc.tensor.transpose(out=flipped[g][:, t, :], in_=normed[g][:, t, :], identity=ident_f32[:])
-            for g in groups:
-                scaled[g] = work.tile([P, P, PACK], F32, name="scaled", bufs=2 * ROUND)
-                nc.vector.tensor_tensor(
-                    out=scaled[g][:],
-                    in0=flipped[g][:].rearrange("p t k -> p k t"),
-                    in1=ln_cols[:, g, :].unsqueeze(1).to_broadcast([P, P, PACK]),
-                    op=ALU.mult,
-                )
+                    nc.tensor.transpose(out=flipped[:, t, :], in_=normed_of_round[r][:, i, t, :], identity=ident_f32[:])
+                flipped_of_round[r].append(flipped)
+
+        def affine(r):
+            rounded = work.tile([P, ROUND, PACK, P], BF16, name="rounded")
+            for i in range(ROUND):
+                g = r * ROUND + i
+                for t in range(PACK):
+                    nc.scalar.activation(
+                        out=rounded[:, i, t, :],
+                        in_=flipped_of_round[r][i][:, t, :],
+                        func=ACT.Identity,
+                        scale=ln_cols[:, g, t : t + 1],
+                        bias=ln_cols[:, D_GROUPS + g, t : t + 1],
+                    )
+            affine_of_round[r] = rounded
+
+        def interleave(r):
             grouped = work.tile([P, ROUND, P, PACK], BF16, name="grouped", align_bytes=64)
-            for g in groups:
-                nc.vector.tensor_tensor(
-                    out=grouped[:, g - r * ROUND, :, :],
-                    in0=scaled[g][:],
-                    in1=ln_cols[:, D_GROUPS + g, :].unsqueeze(1).to_broadcast([P, P, PACK]),
-                    op=ALU.add,
-                )
+            nc.vector.tensor_copy(out=grouped[:], in_=affine_of_round[r][:].rearrange("p g t k -> p g k t"))
             grouped_of_round[r] = grouped
 
         def quantise(r):
@@ -249,29 +266,31 @@ def tile_transformerblock_pb_k_kernel(
             )
 
         def multiply(r):
-            words = chunks[WO_HALVES * A_GROUPS + r]
             for g in range(r * ROUND, (r + 1) * ROUND):
+                words = chunks[(WO_STRETCHES - LEAD) * A_GROUPS + g]
                 for b in range(F // BANK):
                     cols = slice(b * BANK, (b + 1) * BANK)
-                    first = (g - r * ROUND) * F + b * BANK
                     nc.tensor.matmul_mx(
                         out=hid_banks[b][:],
                         lhsT=h_codes[:, g * P : (g + 1) * P].bitcast(FP8X4),
                         lhsT_scale=h_plane[:, g * P : (g + 1) * P],
-                        rhs=words[:, first : first + BANK].bitcast(FP8X4),
+                        rhs=words[:, cols].bitcast(FP8X4),
                         rhs_scale=w1_planes[4 * (g % 4) : P, g // 4, cols],
                         start=(g == 0),
                         stop=(g == D_GROUPS - 1),
                     )
-            load_next_chunk()
+                load_next_chunk()
 
-        for r in range(N_ROUNDS + 2):
-            if r < N_ROUNDS:
-                prepare(r)
-            if 1 <= r <= N_ROUNDS:
+        for r in range(-1, N_ROUNDS + 1):
+            if r >= 1:
+                interleave(r - 1)
+            if r + 1 < N_ROUNDS:
+                normalise(r + 1)
+                flip(r + 1)
+                affine(r + 1)
+            if r >= 1:
                 quantise(r - 1)
-            if r >= 2:
-                multiply(r - 2)
+                multiply(r - 1)
 
         nc.sync.dma_start(out=x_mid_out, in_=x_mid[:])
 

@@ -57,12 +57,12 @@ def tile_transformerblock_pb_k_kernel(
         psum = stack.enter_context(tc.psum_pool(name="psum", bufs=8))
         stack.enter_context(tc.manual_schedule())
 
+        wo_planes = keep.tile([P, A_GROUPS, CHUNK], U8, align_bytes=64)
+        nc.vector.memset(wo_planes[:].bitcast(I32), 0)
         vec_rows = keep.tile([P, BANK], BF16)
         nc.vector.memset(vec_rows[:].bitcast(I32), 0)
         eps_col = keep.tile([P, 1], F32)
         nc.vector.memset(eps_col[:], EPS)
-        wo_planes = keep.tile([P, A_GROUPS, CHUNK], U8, align_bytes=64)
-        nc.vector.memset(wo_planes[:].bitcast(I32), 0)
         w1_planes = keep.tile([P, D_GROUPS // 4, F], U8, align_bytes=64)
         nc.vector.memset(w1_planes[:].bitcast(I32), 0)
         ident_f32 = keep.tile([P, P], F32)
@@ -72,21 +72,20 @@ def tile_transformerblock_pb_k_kernel(
 
         attn_sb = keep.tile([P, A_DIM], BF16)
         nc.sync.dma_start(out=attn_sb[:], in_=attn_rows)
+        wo_planes_i = wo_planes[:].bitcast(I32)
+        for q in (2, 3, 0, 1):
+            for g in range(A_GROUPS):
+                nc.sync.dma_start(
+                    out=wo_planes_i[32 * q : 32 * q + 16, g, :],
+                    in_=wo_scales[g, 4 * q : 4 * q + 4, :].rearrange("r (c n) -> c r n", c=WO_STRETCHES),
+                )
+        x_sb = keep.tile([P, D], BF16)
+        nc.sync.dma_start(out=x_sb[:], in_=x_rows)
         for row, vec in ((ROW_B_OUT, b_out), (ROW_B1, b1), (ROW_GAIN, ln2_g), (ROW_SHIFT, ln2_b)):
             as_rows = vec.rearrange("(r c) -> r c", c=BANK)
             nc.scalar.dma_start(out=vec_rows[row : row + as_rows.shape[0], :], in_=as_rows)
         table_warm = keep.tile([P, 1], F32)
         nc.scalar.activation(out=table_warm[:], in_=eps_col[:], func=ACT.Sqrt)
-        x_sb = keep.tile([P, D], BF16)
-        nc.sync.dma_start(out=x_sb[:], in_=x_rows)
-        wo_planes_i = wo_planes[:].bitcast(I32)
-
-        def load_wo_scales(g):
-            for q in range(4):
-                nc.sync.dma_start(
-                    out=wo_planes_i[32 * q : 32 * q + 16, g, :],
-                    in_=wo_scales[g, 4 * q : 4 * q + 4, :].rearrange("r (c n) -> c r n", c=WO_STRETCHES),
-                )
 
         w1_planes_f = w1_planes[:].bitcast(F32)
         for four in range(D_GROUPS // 4):
@@ -98,7 +97,6 @@ def tile_transformerblock_pb_k_kernel(
 
         lead_words = [keep.tile([P, LEAD * CHUNK], U32, name="lead%d" % g, align_bytes=64) for g in range(A_GROUPS)]
         for g in range(A_GROUPS):
-            load_wo_scales(g)
             nc.sync.dma_start(out=lead_words[g][:].bitcast(I32), in_=wo_words[g, :, : LEAD * CHUNK])
         chunk_sources = [
             wo_words[g, :, c * CHUNK : (c + 1) * CHUNK] for c in range(LEAD, WO_STRETCHES) for g in range(A_GROUPS)

from contextlib import ExitStack

import concourse.mybir as mybir
from concourse.masks import make_identity

F32 = mybir.dt.float32
BF16 = mybir.dt.bfloat16
I32 = mybir.dt.int32
U32 = mybir.dt.uint32
U8 = mybir.dt.uint8
FP8X4 = mybir.dt.float8_e4m3fn_x4
ALU = mybir.AluOpType
ACT = mybir.ActivationFunctionType

P = 128
PACK = 4
K_PASS = P * PACK
BANK = 512
A_DIM = 1024
D = 8192
F = 2048
EPS = 1e-5
A_GROUPS = A_DIM // K_PASS
D_GROUPS = D // K_PASS
CHUNK = 2048
CHUNK_BANKS = CHUNK // BANK
WO_STRETCHES = D // CHUNK
LEAD = 2
W_BUFS = 10
ROUND = 2
N_ROUNDS = D_GROUPS // ROUND
ROW_B_OUT = 0
ROW_B1 = 16
ROW_GAIN = 32
ROW_SHIFT = 48

FLOPS = 2 * P * A_DIM * D + 2 * P * D * F


def tile_transformerblock_pb_k_kernel(
    tc, attn, x, w_out_words, w_out_scales, b_out, ln2_g, ln2_b, w1_words, w1_scales, b1, out_0, out_1
):
    nc = tc.nc
    attn_rows = attn.flatten_outer_dims()
    x_rows = x.flatten_outer_dims()
    x_mid_out = out_0.flatten_outer_dims()
    hid_out = out_1.flatten_outer_dims()
    wo_words = w_out_words.rearrange("g p n t -> g p (n t)").bitcast(I32)
    w1_words_i = w1_words.rearrange("g p n t -> g p (n t)").bitcast(I32)
    wo_scales = w_out_scales.bitcast(I32)
    w1_scales_f = w1_scales.bitcast(F32)

    with ExitStack() as stack:
        keep = stack.enter_context(tc.tile_pool(name="keep", bufs=1))
        weights = stack.enter_context(tc.tile_pool(name="weights", bufs=W_BUFS))
        work = stack.enter_context(tc.tile_pool(name="work", bufs=3))
        psum = stack.enter_context(tc.psum_pool(name="psum", bufs=8))
        stack.enter_context(tc.manual_schedule())

        wo_planes = keep.tile([P, A_GROUPS, CHUNK], U8, align_bytes=64)
        nc.vector.memset(wo_planes[:].bitcast(I32), 0)
        vec_rows = keep.tile([P, BANK], BF16)
        nc.vector.memset(vec_rows[:].bitcast(I32), 0)
        eps_col = keep.tile([P, 1], F32)
        nc.vector.memset(eps_col[:], EPS)
        w1_planes = keep.tile([P, D_GROUPS // 4, F], U8, align_bytes=64)
        nc.vector.memset(w1_planes[:].bitcast(I32), 0)
        ident_f32 = keep.tile([P, P], F32)
        make_identity(nc, ident_f32[:])
        ident_bf = keep.tile([P, P], BF16)
        make_identity(nc, ident_bf[:])

        attn_sb = keep.tile([P, A_DIM], BF16)
        nc.sync.dma_start(out=attn_sb[:], in_=attn_rows)
        wo_planes_i = wo_planes[:].bitcast(I32)
        for q in (2, 3, 0, 1):
            for g in range(A_GROUPS):
                nc.sync.dma_start(
                    out=wo_planes_i[32 * q : 32 * q + 16, g, :],
                    in_=wo_scales[g, 4 * q : 4 * q + 4, :].rearrange("r (c n) -> c r n", c=WO_STRETCHES),
                )
        x_sb = keep.tile([P, D], BF16)
        nc.sync.dma_start(out=x_sb[:], in_=x_rows)
        for row, vec in ((ROW_B_OUT, b_out), (ROW_B1, b1), (ROW_GAIN, ln2_g), (ROW_SHIFT, ln2_b)):
            as_rows = vec.rearrange("(r c) -> r c", c=BANK)
            nc.scalar.dma_start(out=vec_rows[row : row + as_rows.shape[0], :], in_=as_rows)
        table_warm = keep.tile([P, 1], F32)
        nc.scalar.activation(out=table_warm[:], in_=eps_col[:], func=ACT.Sqrt)

        w1_planes_f = w1_planes[:].bitcast(F32)
        for four in range(D_GROUPS // 4):
            for q in range(4):
                nc.gpsimd.dma_start(
                    out=w1_planes_f[32 * q : 32 * q + 16, four, :],
                    in_=w1_scales_f[4 * four : 4 * four + 4, 4 * q : 4 * q + 4, :],
                )

        lead_words = [keep.tile([P, LEAD * CHUNK], U32, name="lead%d" % g, align_bytes=64) for g in range(A_GROUPS)]
        for g in range(A_GROUPS):
            nc.sync.dma_start(out=lead_words[g][:].bitcast(I32), in_=wo_words[g, :, : LEAD * CHUNK])
        chunk_sources = [
            wo_words[g, :, c * CHUNK : (c + 1) * CHUNK] for c in range(LEAD, WO_STRETCHES) for g in range(A_GROUPS)
        ] + [w1_words_i[g] for g in range(D_GROUPS)]
        chunks = []

        def load_next_chunk():
            if len(chunks) < len(chunk_sources):
                words = weights.tile([P, CHUNK], U32, name="words", align_bytes=64)
                nc.sync.dma_start(out=words[:].bitcast(I32), in_=chunk_sources[len(chunks)])
                chunks.append(words)

        for i in range(W_BUFS):
            load_next_chunk()

        attn_words = attn_sb[:].bitcast(F32)
        attn_t = psum.tile([P, A_GROUPS, 2, P], F32, name="attn_t", tag="bank")
        for g in range(A_GROUPS):
            for u in range(2):
                nc.tensor.transpose(
                    out=attn_t[:, g, u, :],
                    in_=attn_words[:, 256 * g + u : 256 * (g + 1) : 2],
                    identity=ident_f32[:],
                )
        attn_grouped = keep.tile([P, A_GROUPS * P * PACK], BF16, align_bytes=64)
        nc.vector.tensor_copy(
            out=attn_grouped[:].bitcast(F32).rearrange("p (g k u) -> p g k u", g=A_GROUPS, u=2),
            in_=attn_t[:].rearrange("p g u k -> p g k u"),
        )
        attn_codes = keep.tile([P, A_GROUPS * P], U32, align_bytes=64)
        attn_plane = keep.tile([P, A_GROUPS * P], U8, align_bytes=64)

        ln_t = psum.tile([P, PACK, P], BF16, name="ln_t", tag="bank")
        for t in range(PACK):
            nc.tensor.transpose(out=ln_t[:, t, :], in_=vec_rows[:, t:BANK:PACK], identity=ident_bf[:])
        ln_cols = keep.tile([P, 2 * D_GROUPS, PACK], F32)
        nc.vector.tensor_copy(
            out=ln_cols[:], in_=ln_t[:, :, ROW_GAIN : ROW_GAIN + 2 * D_GROUPS].rearrange("p t r -> p r t")
        )
        nc.vector.quantize_mx(out=attn_codes[:].bitcast(FP8X4), scales=attn_plane[:], in_=attn_grouped[:])

        def spread_row(bank, row, stop):
            nc.tensor.matmul(
                out=bank[:],
                lhsT=ident_bf[:, row : row + 1].to_broadcast([P, P]),
                rhs=vec_rows[:],
                start=True,
                stop=stop,
            )

        b1_all = keep.tile([P, F], F32)
        for j in range(F // BANK):
            bank = psum.tile([P, BANK], F32, name="spread", tag="bank")
            spread_row(bank, ROW_B1 + j, stop=True)
            nc.scalar.copy(out=b1_all[:, j * BANK : (j + 1) * BANK], in_=bank[:])

        x_mid = keep.tile([P, D], F32)

        def start_x_mid(c):
            for j in range(c * CHUNK_BANKS, (c + 1) * CHUNK_BANKS):
                cols = slice(j * BANK, (j + 1) * BANK)
                bank = psum.tile([P, BANK], F32, name="spread", tag="bank")
                spread_row(bank, ROW_B_OUT + j, stop=False)
                nc.tensor.matmul(out=bank[:], lhsT=ident_bf[:], rhs=x_sb[:, cols], start=False, stop=True)
                nc.scalar.copy(out=x_mid[:, cols], in_=bank[:])

        start_x_mid(0)

        stats = keep.tile([P, D // BANK, 6], F32)
        for c in range(WO_STRETCHES):
            if c + 1 < WO_STRETCHES:
                start_x_mid(c + 1)
            banks = [psum.tile([P, BANK], F32, name="acc%d" % b, tag="bank") for b in range(CHUNK_BANKS)]
            for g in range(A_GROUPS):
                for b in range(CHUNK_BANKS):
                    cols = slice(b * BANK, (b + 1) * BANK)
                    if c < LEAD:
                        rhs = lead_words[g][:, c * CHUNK + b * BANK : c * CHUNK + (b + 1) * BANK]
                    else:
                        rhs = chunks[(c - LEAD) * A_GROUPS + g][:, cols]
                    nc.tensor.matmul_mx(
                        out=banks[b][:],
                        lhsT=attn_codes[:, g * P : (g + 1) * P].bitcast(FP8X4),
                        lhsT_scale=attn_plane[:, g * P : (g + 1) * P],
                        rhs=rhs.bitcast(FP8X4),
                        rhs_scale=wo_planes[4 * c : P, g, cols],
                        start=(g == 0),
                        stop=(g == A_GROUPS - 1),
                    )
                if c >= LEAD:
                    load_next_chunk()
            for b in range(CHUNK_BANKS):
                cols = slice(c * CHUNK + b * BANK, c * CHUNK + (b + 1) * BANK)
                nc.vector.tensor_tensor(out=x_mid[:, cols], in0=banks[b][:], in1=x_mid[:, cols], op=ALU.add)
            for b in range(CHUNK_BANKS):
                cols = slice(c * CHUNK + b * BANK, c * CHUNK + (b + 1) * BANK)
                nc.vector.bn_stats(out=stats[:, c * CHUNK_BANKS + b, :], in_=x_mid[:, cols])

        mean_var = keep.tile([P, 2], F32)
        nc.vector.bn_aggr(out=mean_var[:], in_=stats[:].rearrange("p j s -> p (j s)"))
        std = keep.tile([P, 1], F32)
        nc.scalar.activation(out=std[:], in_=mean_var[:, 1:2], func=ACT.Sqrt, bias=eps_col[:], scale=1.0)
        rstd = keep.tile([P, 1], F32)
        nc.vector.reciprocal(out=rstd[:], in_=std[:])
        minus_mean_rstd = keep.tile([P, 1], F32)
        nc.vector.tensor_scalar(
            out=minus_mean_rstd[:], in0=mean_var[:, 0:1], scalar1=rstd[:, 0:1], scalar2=-1.0, op0=ALU.mult, op1=ALU.mult
        )

        h_codes = keep.tile([P, D_GROUPS * P], U32, align_bytes=64)
        h_plane = keep.tile([P, D_GROUPS * P], U8, align_bytes=64)
        hid_banks = [psum.tile([P, BANK], F32, name="hid%d" % b, tag="bank") for b in range(F // BANK)]
        normed_of_round = {}
        flipped_of_round = {}
        affine_of_round = {}
        grouped_of_round = {}

        def normalise(r):
            normed = work.tile([P, ROUND, PACK, P], F32, name="normed")
            nc.vector.tensor_scalar(
                out=normed[:].rearrange("k g t p -> k g p t"),
                in0=x_mid[:, r * ROUND * K_PASS : (r + 1) * ROUND * K_PASS].rearrange(
                    "k (g p t) -> k g p t", g=ROUND, t=PACK
                ),
                scalar1=rstd[:, 0:1],
                scalar2=minus_mean_rstd[:, 0:1],
                op0=ALU.mult,
                op1=ALU.add,
            )
            normed_of_round[r] = normed

        def flip(r):
            flipped_of_round[r] = []
            for i in range(ROUND):
                flipped = psum.tile([P, PACK, P], F32, name="flipped", tag="bank")
                for t in range(PACK):
                    nc.tensor.transpose(out=flipped[:, t, :], in_=normed_of_round[r][:, i, t, :], identity=ident_f32[:])
                flipped_of_round[r].append(flipped)

        def affine(r):
            rounded = work.tile([P, ROUND, PACK, P], BF16, name="rounded")
            for i in range(ROUND):
                g = r * ROUND + i
                for t in range(PACK):
                    nc.scalar.activation(
                        out=rounded[:, i, t, :],
                        in_=flipped_of_round[r][i][:, t, :],
                        func=ACT.Identity,
                        scale=ln_cols[:, g, t : t + 1],
                        bias=ln_cols[:, D_GROUPS + g, t : t + 1],
                    )
            affine_of_round[r] = rounded

        def interleave(r):
            grouped = work.tile([P, ROUND, P, PACK], BF16, name="grouped", align_bytes=64)
            nc.vector.tensor_copy(out=grouped[:], in_=affine_of_round[r][:].rearrange("p g t k -> p g k t"))
            grouped_of_round[r] = grouped

        def quantise(r):
            cols = slice(r * ROUND * P, (r + 1) * ROUND * P)
            nc.vector.quantize_mx(
                out=h_codes[:, cols].bitcast(FP8X4),
                scales=h_plane[:, cols],
                in_=grouped_of_round[r][:].rearrange("p g k t -> p (g k t)"),
            )

        def multiply(r):
            for g in range(r * ROUND, (r + 1) * ROUND):
                words = chunks[(WO_STRETCHES - LEAD) * A_GROUPS + g]
                for b in range(F // BANK):
                    cols = slice(b * BANK, (b + 1) * BANK)
                    nc.tensor.matmul_mx(
                        out=hid_banks[b][:],
                        lhsT=h_codes[:, g * P : (g + 1) * P].bitcast(FP8X4),
                        lhsT_scale=h_plane[:, g * P : (g + 1) * P],
                        rhs=words[:, cols].bitcast(FP8X4),
                        rhs_scale=w1_planes[4 * (g % 4) : P, g // 4, cols],
                        start=(g == 0),
                        stop=(g == D_GROUPS - 1),
                    )
                load_next_chunk()

        for r in range(-1, N_ROUNDS + 1):
            if r >= 1:
                interleave(r - 1)
            if r + 1 < N_ROUNDS:
                normalise(r + 1)
                flip(r + 1)
                affine(r + 1)
            if r >= 1:
                quantise(r - 1)
                multiply(r - 1)

        nc.sync.dma_start(out=x_mid_out, in_=x_mid[:])

        hid_sb = keep.tile([P, F], F32)
        for b in range(F // BANK):
            cols = slice(b * BANK, (b + 1) * BANK)
            biased = work.tile([P, BANK], F32, name="biased")
            nc.vector.tensor_tensor(out=biased[:], in0=hid_banks[b][:], in1=b1_all[:, cols], op=ALU.add)
            nc.scalar.activation(out=hid_sb[:, cols], in_=biased[:], func=ACT.Gelu)
        nc.sync.dma_start(out=hid_out, in_=hid_sb[:])
